import numpy as np
import ml_dtypes

BF16 = ml_dtypes.bfloat16


def bf(x):
    return np.asarray(x, np.float32).astype(BF16)


def f32(x):
    return np.asarray(x, np.float32)


def f64(x):
    return np.asarray(x).astype(np.float64)


def striped(idx):
    return np.tile(idx.reshape(-1, 16).T, (8, 1))


D, M, S, RUN, K, E, N = 128, 128, 1024, 512, 4, 1024, 2048
CUTOFF = 5.0


def silu(v):
    return v / (1.0 + np.exp(-v))


def setup_inputs():
    return {
        "table": bf(np.random.standard_normal((D, S))),
        "w_src": bf(np.random.standard_normal((D, M)) / np.sqrt(D)),
        "w_dst": bf(np.random.standard_normal((D, M)) / np.sqrt(D)),
        "w_rbf": bf(np.random.standard_normal((D, M)) / np.sqrt(D)),
        "dist": f32(0.5 + 4.0 * np.random.random((1, E))),
        "w0": f32(3.0 * np.random.standard_normal((D, 1))),
        "b0": f32(0.5 * np.random.standard_normal((D, 1))),
        "b": f32(0.2 * np.random.standard_normal((M, 1))),
        "w1": f32(3.0 * np.random.standard_normal((M, 1))),
        "offs": striped(np.concatenate([np.random.permutation(S)[:RUN] for _ in range(K)])),
    }


def reference(table, w_src, w_dst, w_rbf, dist, w0, b0, b, w1, offs):
    idx = offs[:16].T.reshape(-1)
    t = f64(table)
    dd = f64(dist)
    rbf = np.sqrt(2.0 / CUTOFF) * np.sin(dd * (np.pi / CUTOFF)) / dd
    rbf0 = silu(f64(w0) * rbf + f64(b0))
    pre = f64(w_src).T @ t[:, idx[:E]] + f64(w_dst).T @ t[:, idx[E:]] + f64(w_rbf).T @ rbf0 + f64(b)
    return f64(w1) * rbf * silu(pre)

@@ -1,0 +1,98 @@
+import math
+
+import concourse.mybir as mybir
+
+FEATURES = 128
+NODES = 1024
+EDGES = 1024
+PIECE = 256
+PIECES = EDGES // PIECE
+BLOCK = 32
+RUNS = EDGES // BLOCK
+CUTOFF = 5.0
+FLOPS = 2 * 3 * FEATURES * FEATURES * EDGES
+
+BF16, F32, U16 = mybir.dt.bfloat16, mybir.dt.float32, mybir.dt.uint16
+ACT = mybir.ActivationFunctionType
+ALU = mybir.AluOpType
+
+
+def tile_edgefeatureinit_kernel(tc, table, w_src, w_dst, w_rbf, dist, w0, b0, b, w1, offs, out):
+    nc = tc.nc
+    with (
+        tc.tile_pool(name="held", bufs=1) as held,
+        tc.tile_pool(name="work", bufs=4) as work,
+        tc.psum_pool(name="psum", bufs=1) as psum,
+    ):
+        runs = held.tile([FEATURES, BLOCK], F32, name="runs", align_bytes=64)
+        for group in range(FEATURES // BLOCK):
+            queue = nc.sync if group % 2 == 0 else nc.scalar
+            queue.dma_start(runs[group * BLOCK : (group + 1) * BLOCK, :], dist.rearrange("o (k i) -> (o k) i", i=BLOCK))
+        nodes = held.tile([FEATURES, NODES], BF16, name="nodes")
+        nc.scalar.dma_start(nodes[:], table)
+        offsets = held.tile([FEATURES, 2 * EDGES // 16], U16, name="offsets")
+        nc.sync.dma_start(offsets[:], offs)
+        src_weights = held.tile([FEATURES, FEATURES], BF16, name="src_weights")
+        nc.sync.dma_start(src_weights[:], w_src)
+        dst_weights = held.tile([FEATURES, FEATURES], BF16, name="dst_weights")
+        nc.sync.dma_start(dst_weights[:], w_dst)
+        w0_col = held.tile([FEATURES, 1], F32, name="w0_col")
+        nc.sync.dma_start(w0_col[:], w0)
+        b0_col = held.tile([FEATURES, 1], F32, name="b0_col")
+        nc.sync.dma_start(b0_col[:], b0)
+        rbf_weights = held.tile([FEATURES, FEATURES], BF16, name="rbf_weights")
+        nc.sync.dma_start(rbf_weights[:], w_rbf)
+        b_col = held.tile([FEATURES, 1], F32, name="b_col")
+        nc.sync.dma_start(b_col[:], b)
+        w1_col = held.tile([FEATURES, 1], F32, name="w1_col")
+        nc.sync.dma_start(w1_col[:], w1)
+
+        scratch = held.tile([FEATURES, 1], F32, name="scratch")
+        nc.vector.memset(scratch[:], 0.0)
+        nc.scalar.activation(scratch[:], scratch[:], ACT.Silu)
+
+        lengths = held.tile([FEATURES, RUNS], F32, name="lengths", align_bytes=64)
+        nc.vector.transpose(lengths[:], runs[:])
+
+        sine = held.tile([FEATURES, RUNS], F32, name="sine")
+        nc.scalar.activation(sine[:], lengths[:], ACT.Sin, scale=math.pi / CUTOFF)
+        inverse = held.tile([FEATURES, RUNS], F32, name="inverse")
+        nc.vector.reciprocal(inverse[:], lengths[:])
+
+        wide = [FEATURES, PIECE // BLOCK, BLOCK]
+        repeats = []
+        for step in range(PIECES + 1):
+            if step < PIECES:
+                piece_runs = slice(step * (PIECE // BLOCK), (step + 1) * (PIECE // BLOCK))
+                repeated = work.tile(wide, F32, name="repeated", align_bytes=64)
+                nc.vector.scalar_tensor_tensor(
+                    repeated[:],
+                    sine[:, piece_runs].unsqueeze(2).to_broadcast(wide),
+                    math.sqrt(2.0 / CUTOFF),
+                    inverse[:, piece_runs].unsqueeze(2).to_broadcast(wide),
+                    ALU.mult,
+                    ALU.mult,
+                )
+                repeats.append(repeated)
+            if step == 0:
+                continue
+            piece = step - 1
+            edges = slice(piece * PIECE, (piece + 1) * PIECE)
+            src_list = offsets[:, piece * (PIECE // 16) : (piece + 1) * (PIECE // 16)]
+            dst_list = offsets[:, (EDGES + piece * PIECE) // 16 : (EDGES + (piece + 1) * PIECE) // 16]
+
+            rbf = work.tile([FEATURES, PIECE], F32, name="rbf", align_bytes=64)
+            nc.vector.transpose(rbf[:], repeats[piece][:].rearrange("p k i -> p (k i)"))
+
+            pre = psum.tile([FEATURES, PIECE], F32, name=f"pre{piece}")
+            nc.tensor.matmul(pre[:], src_weights[:], nodes[:].indirect(src_list), start=True, stop=False)
+            nc.tensor.matmul(pre[:], dst_weights[:], nodes[:].indirect(dst_list), start=False, stop=False)
+            rbf0 = work.tile([FEATURES, PIECE], BF16, name="rbf0")
+            nc.scalar.activation(rbf0[:], rbf[:], ACT.Silu, bias=b0_col[:], scale=w0_col[:])
+            nc.tensor.matmul(pre[:], rbf_weights[:], rbf0[:], start=False, stop=True)
+
+            gated = work.tile([FEATURES, PIECE], F32, name="gated")
+            nc.scalar.activation(gated[:], pre[:], ACT.Silu, bias=b_col[:])
+            result = work.tile([FEATURES, PIECE], F32, name="result")
+            nc.vector.scalar_tensor_tensor(result[:], gated[:], w1_col[:], rbf[:], ALU.mult, ALU.mult)
+            nc.sync.dma_start(out[:, edges], result[:])

@@ -59,24 +59,23 @@ def tile_edgefeatureinit_kernel(tc, table, w_src, w_dst, w_rbf, dist, w0, b0, b,
         inverse = held.tile([FEATURES, RUNS], F32, name="inverse")
         nc.vector.reciprocal(inverse[:], lengths[:])
 
+        quotient = held.tile([FEATURES, RUNS], F32, name="quotient")
+        nc.vector.tensor_tensor(quotient[:], sine[:], inverse[:], ALU.mult)
+
         wide = [FEATURES, PIECE // BLOCK, BLOCK]
+        norm = math.sqrt(2.0 / CUTOFF)
         repeats = []
-        for step in range(PIECES + 1):
-            if step < PIECES:
-                piece_runs = slice(step * (PIECE // BLOCK), (step + 1) * (PIECE // BLOCK))
-                repeated = work.tile(wide, F32, name="repeated", align_bytes=64)
-                nc.vector.scalar_tensor_tensor(
-                    repeated[:],
-                    sine[:, piece_runs].unsqueeze(2).to_broadcast(wide),
-                    math.sqrt(2.0 / CUTOFF),
-                    inverse[:, piece_runs].unsqueeze(2).to_broadcast(wide),
-                    ALU.mult,
-                    ALU.mult,
-                )
-                repeats.append(repeated)
-            if step == 0:
-                continue
-            piece = step - 1
+        for piece in range(PIECES):
+            piece_runs = slice(piece * (PIECE // BLOCK), (piece + 1) * (PIECE // BLOCK))
+            once = quotient[:, piece_runs].unsqueeze(2).to_broadcast(wide)
+            repeated = work.tile(wide, F32, name="repeated", align_bytes=64)
+            if piece == 1:
+                nc.scalar.activation(repeated[:], once, ACT.Copy, scale=norm)
+            else:
+                nc.vector.tensor_scalar(repeated[:], once, norm, None, ALU.mult)
+            repeats.append(repeated)
+
+        for piece in range(PIECES):
             edges = slice(piece * PIECE, (piece + 1) * PIECE)
             src_list = offsets[:, piece * (PIECE // 16) : (piece + 1) * (PIECE // 16)]
             dst_list = offsets[:, (EDGES + piece * PIECE) // 16 : (EDGES + (piece + 1) * PIECE) // 16]

@@ -34,18 +34,27 @@ def tile_edgefeatureinit_kernel(tc, table, w_src, w_dst, w_rbf, dist, w0, b0, b,
         nc.sync.dma_start(offsets[:], offs)
         src_weights = held.tile([FEATURES, FEATURES], BF16, name="src_weights")
         nc.sync.dma_start(src_weights[:], w_src)
-        dst_weights = held.tile([FEATURES, FEATURES], BF16, name="dst_weights")
-        nc.sync.dma_start(dst_weights[:], w_dst)
         w0_col = held.tile([FEATURES, 1], F32, name="w0_col")
         nc.sync.dma_start(w0_col[:], w0)
         b0_col = held.tile([FEATURES, 1], F32, name="b0_col")
-        nc.sync.dma_start(b0_col[:], b0)
+        nc.gpsimd.dma_start(b0_col[:], b0)
+        dst_weights = held.tile([FEATURES, FEATURES], BF16, name="dst_weights")
+        nc.sync.dma_start(dst_weights[:], w_dst)
         rbf_weights = held.tile([FEATURES, FEATURES], BF16, name="rbf_weights")
         nc.sync.dma_start(rbf_weights[:], w_rbf)
         b_col = held.tile([FEATURES, 1], F32, name="b_col")
         nc.sync.dma_start(b_col[:], b)
         w1_col = held.tile([FEATURES, 1], F32, name="w1_col")
         nc.sync.dma_start(w1_col[:], w1)
+
+        columns = PIECE // 16
+        pres = [psum.tile([FEATURES, PIECE], F32, name=f"pre{piece}") for piece in range(PIECES)]
+        for piece, pre in enumerate(pres):
+            src_list = offsets[:, piece * columns : (piece + 1) * columns]
+            nc.tensor.matmul(pre[:], src_weights[:], nodes[:].indirect(src_list), start=True, stop=False)
+        for piece, pre in enumerate(pres):
+            dst_list = offsets[:, (PIECES + piece) * columns : (PIECES + piece + 1) * columns]
+            nc.tensor.matmul(pre[:], dst_weights[:], nodes[:].indirect(dst_list), start=False, stop=False)
 
         scratch = held.tile([FEATURES, 1], F32, name="scratch")
         nc.vector.memset(scratch[:], 0.0)
@@ -77,15 +86,10 @@ def tile_edgefeatureinit_kernel(tc, table, w_src, w_dst, w_rbf, dist, w0, b0, b,
 
         for piece in range(PIECES):
             edges = slice(piece * PIECE, (piece + 1) * PIECE)
-            src_list = offsets[:, piece * (PIECE // 16) : (piece + 1) * (PIECE // 16)]
-            dst_list = offsets[:, (EDGES + piece * PIECE) // 16 : (EDGES + (piece + 1) * PIECE) // 16]
-
             rbf = work.tile([FEATURES, PIECE], F32, name="rbf", align_bytes=64)
             nc.vector.transpose(rbf[:], repeats[piece][:].rearrange("p k i -> p (k i)"))
 
-            pre = psum.tile([FEATURES, PIECE], F32, name=f"pre{piece}")
-            nc.tensor.matmul(pre[:], src_weights[:], nodes[:].indirect(src_list), start=True, stop=False)
-            nc.tensor.matmul(pre[:], dst_weights[:], nodes[:].indirect(dst_list), start=False, stop=False)
+            pre = pres[piece]
             rbf0 = work.tile([FEATURES, PIECE], BF16, name="rbf0")
             nc.scalar.activation(rbf0[:], rbf[:], ACT.Silu, bias=b0_col[:], scale=w0_col[:])
             nc.tensor.matmul(pre[:], rbf_weights[:], rbf0[:], start=False, stop=True)

@@ -69,19 +69,29 @@ def tile_edgefeatureinit_kernel(tc, table, w_src, w_dst, w_rbf, dist, w0, b0, b,
         nc.vector.reciprocal(inverse[:], lengths[:])
 
         quotient = held.tile([FEATURES, RUNS], F32, name="quotient")
-        nc.vector.tensor_tensor(quotient[:], sine[:], inverse[:], ALU.mult)
 
         wide = [FEATURES, PIECE // BLOCK, BLOCK]
         norm = math.sqrt(2.0 / CUTOFF)
         repeats = []
         for piece in range(PIECES):
             piece_runs = slice(piece * (PIECE // BLOCK), (piece + 1) * (PIECE // BLOCK))
-            once = quotient[:, piece_runs].unsqueeze(2).to_broadcast(wide)
             repeated = work.tile(wide, F32, name="repeated", align_bytes=64)
-            if piece == 1:
-                nc.scalar.activation(repeated[:], once, ACT.Copy, scale=norm)
+            if piece == 0:
+                nc.vector.scalar_tensor_tensor(
+                    repeated[:],
+                    sine[:, piece_runs].unsqueeze(2).to_broadcast(wide),
+                    norm,
+                    inverse[:, piece_runs].unsqueeze(2).to_broadcast(wide),
+                    ALU.mult,
+                    ALU.mult,
+                )
+                nc.vector.tensor_tensor(quotient[:], sine[:], inverse[:], ALU.mult)
             else:
-                nc.vector.tensor_scalar(repeated[:], once, norm, None, ALU.mult)
+                once = quotient[:, piece_runs].unsqueeze(2).to_broadcast(wide)
+                if piece == 1:
+                    nc.scalar.activation(repeated[:], once, ACT.Copy, scale=norm)
+                else:
+                    nc.vector.tensor_scalar(repeated[:], once, norm, None, ALU.mult)
             repeats.append(repeated)
 
         for piece in range(PIECES):

@@ -88,7 +88,7 @@ def tile_edgefeatureinit_kernel(tc, table, w_src, w_dst, w_rbf, dist, w0, b0, b,
                 nc.vector.tensor_tensor(quotient[:], sine[:], inverse[:], ALU.mult)
             else:
                 once = quotient[:, piece_runs].unsqueeze(2).to_broadcast(wide)
-                if piece == 1:
+                if piece in (1, 2):
                     nc.scalar.activation(repeated[:], once, ACT.Copy, scale=norm)
                 else:
                     nc.vector.tensor_scalar(repeated[:], once, norm, None, ALU.mult)

import math

import concourse.mybir as mybir

FEATURES = 128
NODES = 1024
EDGES = 1024
PIECE = 256
PIECES = EDGES // PIECE
BLOCK = 32
RUNS = EDGES // BLOCK
CUTOFF = 5.0
FLOPS = 2 * 3 * FEATURES * FEATURES * EDGES

BF16, F32, U16 = mybir.dt.bfloat16, mybir.dt.float32, mybir.dt.uint16
ACT = mybir.ActivationFunctionType
ALU = mybir.AluOpType


def tile_edgefeatureinit_kernel(tc, table, w_src, w_dst, w_rbf, dist, w0, b0, b, w1, offs, out):
    nc = tc.nc
    with (
        tc.tile_pool(name="held", bufs=1) as held,
        tc.tile_pool(name="work", bufs=4) as work,
        tc.psum_pool(name="psum", bufs=1) as psum,
    ):
        runs = held.tile([FEATURES, BLOCK], F32, name="runs", align_bytes=64)
        for group in range(FEATURES // BLOCK):
            queue = nc.sync if group % 2 == 0 else nc.scalar
            queue.dma_start(runs[group * BLOCK : (group + 1) * BLOCK, :], dist.rearrange("o (k i) -> (o k) i", i=BLOCK))
        nodes = held.tile([FEATURES, NODES], BF16, name="nodes")
        nc.scalar.dma_start(nodes[:], table)
        offsets = held.tile([FEATURES, 2 * EDGES // 16], U16, name="offsets")
        nc.sync.dma_start(offsets[:], offs)
        src_weights = held.tile([FEATURES, FEATURES], BF16, name="src_weights")
        nc.sync.dma_start(src_weights[:], w_src)
        w0_col = held.tile([FEATURES, 1], F32, name="w0_col")
        nc.sync.dma_start(w0_col[:], w0)
        b0_col = held.tile([FEATURES, 1], F32, name="b0_col")
        nc.gpsimd.dma_start(b0_col[:], b0)
        dst_weights = held.tile([FEATURES, FEATURES], BF16, name="dst_weights")
        nc.sync.dma_start(dst_weights[:], w_dst)
        rbf_weights = held.tile([FEATURES, FEATURES], BF16, name="rbf_weights")
        nc.sync.dma_start(rbf_weights[:], w_rbf)
        b_col = held.tile([FEATURES, 1], F32, name="b_col")
        nc.sync.dma_start(b_col[:], b)
        w1_col = held.tile([FEATURES, 1], F32, name="w1_col")
        nc.sync.dma_start(w1_col[:], w1)

        columns = PIECE // 16
        pres = [psum.tile([FEATURES, PIECE], F32, name=f"pre{piece}") for piece in range(PIECES)]
        for piece, pre in enumerate(pres):
            src_list = offsets[:, piece * columns : (piece + 1) * columns]
            nc.tensor.matmul(pre[:], src_weights[:], nodes[:].indirect(src_list), start=True, stop=False)
        for piece, pre in enumerate(pres):
            dst_list = offsets[:, (PIECES + piece) * columns : (PIECES + piece + 1) * columns]
            nc.tensor.matmul(pre[:], dst_weights[:], nodes[:].indirect(dst_list), start=False, stop=False)

        scratch = held.tile([FEATURES, 1], F32, name="scratch")
        nc.vector.memset(scratch[:], 0.0)
        nc.scalar.activation(scratch[:], scratch[:], ACT.Silu)

        lengths = held.tile([FEATURES, RUNS], F32, name="lengths", align_bytes=64)
        nc.vector.transpose(lengths[:], runs[:])

        sine = held.tile([FEATURES, RUNS], F32, name="sine")
        nc.scalar.activation(sine[:], lengths[:], ACT.Sin, scale=math.pi / CUTOFF)
        inverse = held.tile([FEATURES, RUNS], F32, name="inverse")
        nc.vector.reciprocal(inverse[:], lengths[:])

        quotient = held.tile([FEATURES, RUNS], F32, name="quotient")

        wide = [FEATURES, PIECE // BLOCK, BLOCK]
        norm = math.sqrt(2.0 / CUTOFF)
        repeats = []
        for piece in range(PIECES):
            piece_runs = slice(piece * (PIECE // BLOCK), (piece + 1) * (PIECE // BLOCK))
            repeated = work.tile(wide, F32, name="repeated", align_bytes=64)
            if piece == 0:
                nc.vector.scalar_tensor_tensor(
                    repeated[:],
                    sine[:, piece_runs].unsqueeze(2).to_broadcast(wide),
                    norm,
                    inverse[:, piece_runs].unsqueeze(2).to_broadcast(wide),
                    ALU.mult,
                    ALU.mult,
                )
                nc.vector.tensor_tensor(quotient[:], sine[:], inverse[:], ALU.mult)
            else:
                once = quotient[:, piece_runs].unsqueeze(2).to_broadcast(wide)
                if piece in (1, 2):
                    nc.scalar.activation(repeated[:], once, ACT.Copy, scale=norm)
                else:
                    nc.vector.tensor_scalar(repeated[:], once, norm, None, ALU.mult)
            repeats.append(repeated)

        for piece in range(PIECES):
            edges = slice(piece * PIECE, (piece + 1) * PIECE)
            rbf = work.tile([FEATURES, PIECE], F32, name="rbf", align_bytes=64)
            nc.vector.transpose(rbf[:], repeats[piece][:].rearrange("p k i -> p (k i)"))

            pre = pres[piece]
            rbf0 = work.tile([FEATURES, PIECE], BF16, name="rbf0")
            nc.scalar.activation(rbf0[:], rbf[:], ACT.Silu, bias=b0_col[:], scale=w0_col[:])
            nc.tensor.matmul(pre[:], rbf_weights[:], rbf0[:], start=False, stop=True)

            gated = work.tile([FEATURES, PIECE], F32, name="gated")
            nc.scalar.activation(gated[:], pre[:], ACT.Silu, bias=b_col[:])
            result = work.tile([FEATURES, PIECE], F32, name="result")
            nc.vector.scalar_tensor_tensor(result[:], gated[:], w1_col[:], rbf[:], ALU.mult, ALU.mult)
            nc.sync.dma_start(out[:, edges], result[:])
